import numpy as np
import ml_dtypes


def mxq(x, axis, fmt="e4m3"):
    dtype, down = {"e4m3": (ml_dtypes.float8_e4m3fn, 7), "e5m2": (ml_dtypes.float8_e5m2, 14)}[fmt]
    v = np.moveaxis(np.asarray(x, np.float32).astype(ml_dtypes.bfloat16).astype(np.float64), axis, -1)
    blocks = v.reshape(v.shape[:-1] + (-1, 32))
    amax = np.abs(blocks).max(-1, keepdims=True)
    byte = np.maximum(np.where(amax > 0, np.frexp(amax)[1] - 1 + 127, 0) - down, 1)
    scale = np.exp2(byte - 127.0)
    codes = (blocks / scale).astype(np.float32).astype(dtype).astype(np.float64)
    return np.moveaxis((codes * scale).reshape(v.shape), -1, axis)


WIDE = False


def mx_kscale(k):
    if not WIDE:
        return np.ones(k)
    levels = np.array([10, -10, 5, -5, 0])
    a = np.random.permutation(np.resize(levels, k // 512 * 4)).reshape(k // 512, 4)
    idx = np.arange(k)
    return np.exp2(a[idx // 512, idx % 128 // 32])


BF16 = ml_dtypes.bfloat16


def bf(x):
    return np.asarray(x, np.float32).astype(BF16)


def f64(x):
    return np.asarray(x).astype(np.float64)


B, S, F, U = 4, 1024, 256, 1024
K = 2 * F
TWO_PI = 2.0 * np.pi


def setup_inputs():
    s = mx_kscale(K)[:F]
    u = s / s.max()
    r = np.minimum(1.0, 8.0 * u)
    g = np.concatenate([r, r * r])
    return {"x": bf(np.random.standard_normal((B, S, F)) * u),
            "W": bf(np.random.standard_normal((K, U)) / np.sqrt(K) / g[:, None]),
            "b": bf(np.random.standard_normal(U) * 0.1)}


def reference(x, W, b):
    qp = f64(x) * TWO_PI
    quantum_enhanced = np.tanh(qp) + 0.1 * (np.sin(qp) * np.cos(qp * 0.5))
    entanglement = quantum_enhanced * quantum_enhanced
    feats = np.concatenate([quantum_enhanced, entanglement], axis=-1)
    return np.tanh((mxq(feats, 2, "e4m3") @ mxq(f64(W), 0, "e4m3")) + f64(b))

import math
from contextlib import ExitStack

import concourse.mybir as mybir
from concourse.masks import make_identity

F32 = mybir.dt.float32
BF16 = mybir.dt.bfloat16
I32 = mybir.dt.int32
U32 = mybir.dt.uint32
U8 = mybir.dt.uint8
FP8X4 = mybir.dt.float8_e4m3fn_x4
ACT = mybir.ActivationFunctionType
ALU = mybir.AluOpType

P = 128
TOKENS = 4096
FEAT = 256
UNITS = 1024
NT = TOKENS // P
NCH = 8
CW = 1024
HALF = 64
NB = 512
NA = 6

FLOPS = 2 * TOKENS * 2 * FEAT * UNITS

PIN = True
Q_ON_G = False
SQ_ON_G = False
R1V = 1
LZ, LB, LF, LR, LR1 = 1, 2, 3, 4, 5


def tile_quantumprocessinglayer_t_kernel(tc, x, W, b, out):
    nc = tc.nc
    x_v = x.flatten_outer_dims().rearrange("(p j) f -> p (j f)", j=NT)
    out_v = out.flatten_outer_dims().rearrange("(p j) u -> p j u", j=NT)

    with ExitStack() as ctx:
        keep = ctx.enter_context(tc.tile_pool(name="keep", bufs=1))
        work = ctx.enter_context(tc.tile_pool(name="work", bufs=4))
        outp = ctx.enter_context(tc.tile_pool(name="outp", bufs=6))
        ps_t = ctx.enter_context(tc.psum_pool(name="ps_t", bufs=1))
        ps_a = ctx.enter_context(tc.psum_pool(name="ps_a", bufs=NA))
        if PIN:
            ctx.enter_context(tc.manual_schedule())

        warm = keep.tile([P, 1], F32, name="warm")
        ident = keep.tile([P, P], F32, name="ident")
        x_sb = keep.tile([P, NT * FEAT], BF16, name="x_sb")
        r_sb = keep.tile([P, NT * FEAT], BF16, name="r_sb")
        bias = keep.tile([P, UNITS], BF16, name="bias")
        wraw = {}
        wg = {}
        wc = {}
        ws = {}
        for w in "ab":
            wraw[w] = keep.tile([P, 4 * UNITS], BF16, name="wraw_" + w)
            wg[w] = keep.tile([P, 4 * UNITS], BF16, name="wg_" + w, align_bytes=64)
            wc[w] = keep.tile([P, UNITS], U32, name="wc_" + w, align_bytes=64)
            ws[w] = keep.tile([P, UNITS], U8, name="ws_" + w, align_bytes=64)
        c_lo_q = keep.tile([P, UNITS], U32, name="c_lo_q", align_bytes=64)
        c_hi_s = keep.tile([P, UNITS], U32, name="c_hi_s", align_bytes=64)
        c_lo_s = keep.tile([P, UNITS], U32, name="c_lo_s", align_bytes=64)
        c_hi_q = keep.tile([P, UNITS], U32, name="c_hi_q", align_bytes=64)

        nc.sync.dma_start(out=x_sb[:, 0:CW], in_=x_v[:, 0:CW])
        nc.sync.dma_start(out=wraw["a"][:], in_=W.rearrange("(p j) u -> p (j u)", j=4))
        nc.sync.dma_start(out=x_sb[:, CW : 2 * CW], in_=x_v[:, CW : 2 * CW])
        w_h = W.rearrange("(h p j) u -> h p (j u)", h=2, j=4)
        nc.scalar.dma_start(out=wraw["b"][0:HALF, :], in_=w_h[1])
        nc.scalar.dma_start(out=wraw["b"][HALF:P, :], in_=w_h[0])
        nc.sync.dma_start(out=x_sb[:, 2 * CW : 4 * CW], in_=x_v[:, 2 * CW : 4 * CW])
        nc.sync.dma_start(out=x_sb[:, 4 * CW : 8 * CW], in_=x_v[:, 4 * CW : 8 * CW])
        nc.scalar.dma_start(out=bias[:], in_=b.partition_broadcast(P))

        nc.vector.memset(warm[:], 0.0)
        nc.scalar.activation(out=warm[:], in_=warm[:], func=ACT.Silu)
        make_identity(nc, ident[:])
        nc.vector.memset(c_lo_q[HALF:P, :].bitcast(I32), 0)
        nc.vector.memset(c_lo_s[HALF:P, :].bitcast(I32), 0)
        nc.vector.memset(c_hi_q[0:HALF, :].bitcast(I32), 0)
        nc.vector.memset(c_hi_s[0:HALF, :].bitcast(I32), 0)

        w_ops = (
            (c_lo_q, ws["a"], c_lo_s, ws["b"]),
            (c_hi_q, ws["b"], c_hi_s, ws["a"]),
        )

        def w_regroup(w, eng):
            dst = wg[w][:].rearrange("p (c i t) -> p c t i", i=4, t=4)
            src = wraw[w][:].rearrange("p (t c i) -> p c t i", t=4, i=4)
            if eng == "V":
                nc.vector.tensor_copy(out=dst, in_=src)
            elif eng == "S":
                nc.scalar.copy(out=dst, in_=src)
            else:
                nc.gpsimd.tensor_scalar(out=dst, in0=src, scalar1=1.0, scalar2=0.0, op0=ALU.mult, op1=ALU.add)

        def w_quant(w):
            nc.vector.quantize_mx(out=wc[w][:].bitcast(FP8X4), scales=ws[w][:], in_=wg[w][:])

        def w_split(w):
            lo, hi = (c_lo_q, c_hi_s) if w == "a" else (c_lo_s, c_hi_q)
            nc.vector.tensor_copy(out=lo[0:HALF, :].bitcast(I32), in_=wc[w][0:HALF, :].bitcast(I32))
            nc.vector.tensor_copy(out=hi[HALF:P, :].bitcast(I32), in_=wc[w][HALF:P, :].bitcast(I32))

        w_plan = {
            (-4, "b"): (lambda: w_regroup("a", "V"),),
            (-3, "a"): (lambda: w_quant("a"), lambda: w_split("a")),
            (-3, "s"): (lambda: w_regroup("b", "S"),),
            (-2, "a"): (lambda: w_quant("b"),),
            (-2, "b"): (lambda: w_split("b"),),
        }

        def w_step(i, slot):
            for fn in w_plan.get((i, slot), ()):
                fn()

        xw = x_sb[:].bitcast(F32)
        rw = r_sb[:].bitcast(F32)
        n_t = {}
        xt_t = {}
        rt_t = {}
        t_t = {}
        s_t = {}
        a_t = {}
        fe_t = {}
        fc_t = {}
        fs_t = {}
        acc_t = {}
        o_t = {}

        def ok(c):
            return 0 <= c < NCH

        def cols(c):
            return slice(c * CW, (c + 1) * CW)

        def st_r1(c, eng):
            n_t[c] = work.tile([P, CW], I32, name="n_i", bufs=3)
            e = nc.vector if eng == "V" else nc.gpsimd
            e.tensor_scalar(out=n_t[c][:], in0=x_sb[:, cols(c)], scalar1=0.5, scalar2=0.0, op0=ALU.mult, op1=ALU.add)

        def st_r2(c):
            nc.vector.scalar_tensor_tensor(
                out=r_sb[:, cols(c)], in0=n_t[c][:], scalar=-2.0, in1=x_sb[:, cols(c)], op0=ALU.mult, op1=ALU.add
            )

        def transposes(dst, src, c):
            for eo in range(2):
                for pl in range(2):
                    pair = 2 * c + pl
                    nc.tensor.transpose(
                        dst[:, eo * 256 + pl * P : eo * 256 + (pl + 1) * P],
                        src[:, 256 * pair + eo : 256 * (pair + 1) : 2],
                        ident[:],
                    )

        def st_tx(c):
            xt_t[c] = ps_t.tile([P, NB], F32, name="xt")
            transposes(xt_t[c], xw, c)

        def st_tr(c):
            rt_t[c] = ps_t.tile([P, NB], F32, name="rt")
            transposes(rt_t[c], rw, c)

        def from_bank(bank):
            return bank[:].bitcast(BF16).rearrange("p (eo c e) -> p c eo e", eo=2, e=2)

        def grouped(t):
            return t[:].rearrange("p (c eo e) -> p c eo e", eo=2, e=2)

        def st_front(c):
            t_t[c] = work.tile([P, CW], F32, name="t_t")
            s_t[c] = work.tile([P, CW], F32, name="s_t", bufs=3)
            a_t[c] = work.tile([P, CW], F32, name="a_t", bufs=3)
            nc.scalar.activation(out=grouped(t_t[c]), in_=from_bank(xt_t[c]), func=ACT.Tanh, scale=2.0 * math.pi)
            nc.scalar.activation(out=grouped(s_t[c]), in_=from_bank(rt_t[c]), func=ACT.Sin, scale=math.pi)
            nc.scalar.activation(out=a_t[c][:], in_=s_t[c][:], func=ACT.Square, scale=math.sqrt(0.2))

        def st_b(c):
            nc.vector.scalar_tensor_tensor(
                out=a_t[c][:], in0=a_t[c][:], scalar=-0.2, in1=s_t[c][:], op0=ALU.add, op1=ALU.mult
            )

        def st_q(c):
            e = nc.gpsimd if Q_ON_G else nc.vector
            e.tensor_tensor(out=t_t[c][:], in0=t_t[c][:], in1=a_t[c][:], op=ALU.subtract)

        def st_qb(c):
            fe_t[c] = work.tile([P, 2 * CW], BF16, name="fe", bufs=3, align_bytes=64)
            nc.gpsimd.tensor_scalar(
                out=fe_t[c][:, 0:CW], in0=t_t[c][:], scalar1=1.0, scalar2=0.0, op0=ALU.mult, op1=ALU.add
            )

        def st_sq(c):
            if SQ_ON_G:
                nc.gpsimd.tensor_tensor(out=fe_t[c][:, CW : 2 * CW], in0=t_t[c][:], in1=t_t[c][:], op=ALU.mult)
            else:
                nc.scalar.activation(out=fe_t[c][:, CW : 2 * CW], in_=t_t[c][:], func=ACT.Square)

        def st_z(c):
            fc_t[c] = work.tile([P, 2 * CW // 4], U32, name="fc", align_bytes=64)
            fs_t[c] = work.tile([P, 2 * CW // 4], U8, name="fs", align_bytes=64)
            nc.vector.quantize_mx(out=fc_t[c][:].bitcast(FP8X4), scales=fs_t[c][:], in_=fe_t[c][:])

        def st_mm(g):
            c, j = divmod(g, 8)
            if not ok(c):
                return
            pl, hp, h = j // 4, (j // 2) % 2, j % 2
            q_sl = slice(pl * P, (pl + 1) * P)
            s_sl = slice(256 + pl * P, 256 + (pl + 1) * P)
            n_sl = slice(h * NB, (h + 1) * NB)
            cq, pq, cs, psq = w_ops[hp]
            acc = ps_a.tile([P, NB], F32, name="acc")
            acc_t[g] = acc
            nc.tensor.matmul_mx(
                out=acc[:],
                lhsT=fc_t[c][:, q_sl].bitcast(FP8X4),
                lhsT_scale=fs_t[c][:, q_sl],
                rhs=cq[:, n_sl].bitcast(FP8X4),
                rhs_scale=pq[:, n_sl],
                start=True,
                stop=False,
            )
            nc.tensor.matmul_mx(
                out=acc[:],
                lhsT=fc_t[c][:, s_sl].bitcast(FP8X4),
                lhsT_scale=fs_t[c][:, s_sl],
                rhs=cs[:, n_sl].bitcast(FP8X4),
                rhs_scale=psq[:, n_sl],
                start=False,
                stop=True,
            )

        def st_final(c, j):
            g = 8 * c + j
            pl, hp, h = j // 4, (j // 2) % 2, j % 2
            pair = 2 * c + pl
            n_sl = slice(h * NB, (h + 1) * NB)
            if j % 4 == 0:
                o_t[pair] = outp.tile([P, 2, UNITS], F32, name="o_t")
            o = o_t[pair]
            nc.vector.tensor_tensor(out=o[:, hp, n_sl], in0=acc_t[g][:], in1=bias[:, n_sl], op=ALU.add)
            st_mm(g + NA)
            if h == 1:
                nc.scalar.activation(out=o[:, hp, :], in_=o[:, hp, :], func=ACT.Tanh)
            if j % 4 == 3:
                nc.sync.dma_start(out=out_v[:, 2 * pair : 2 * pair + 2, :], in_=o[:])

        for c in range(R1V):
            st_r1(c, "V")
        for i in range(-LR, NCH):
            w_step(i, "a")
            if ok(i + LZ):
                st_z(i + LZ)
            if i + LZ == 0:
                for g in range(NA):
                    st_mm(g)
            if ok(i + LR):
                st_r2(i + LR)
            if ok(i + LB):
                st_b(i + LB)
                st_q(i + LB)
            w_step(i, "b")
            if ok(i + LF):
                st_front(i + LF)
            w_step(i, "s")
            if ok(i + LB):
                st_qb(i + LB)
                st_sq(i + LB)
            if ok(i + LR1) and i + LR1 >= R1V:
                st_r1(i + LR1, "G")
            if ok(i + LR):
                st_tx(i + LR)
                st_tr(i + LR)
            if ok(i):
                for j in range(8):
                    st_final(i, j)
            w_step(i, "c")
